import numpy as np
import ml_dtypes

BF16 = ml_dtypes.bfloat16


def bf(x):
    return np.asarray(x, np.float32).astype(BF16)


def f32(x):
    return np.asarray(x, np.float32)


def f64(x):
    return np.asarray(x).astype(np.float64)


def striped(idx):
    return np.tile(idx.reshape(-1, 16).T, (8, 1))


E, S, M, N = 128, 4096, 256, 1024


def setup_inputs():
    table = np.random.standard_normal((E, S)) * (0.5 + 1.5 * np.random.random_sample((1, S)))
    return {'table': bf(table), 'w': bf(np.random.standard_normal((E, M))), 'b': f32(0.1 * np.random.standard_normal((M, 1))), 'offs': striped(np.random.permutation(np.tile(np.arange(S), 2))[:N])}


def reference(table, w, b, offs):
    idx = offs[:16].T.reshape(-1)
    t = f64(table)
    tn = t / np.sqrt(np.sum(t * t, axis=0, keepdims=True))
    return np.tanh(f64(w).T @ tn[:, idx] + f64(b))

@@ -1,0 +1,64 @@
+import concourse.mybir as mybir
+
+E, S, M, N = 128, 4096, 256, 1024
+P = 128
+BANK = 512
+FLOPS = 2 * E * M * N
+
+BF16, F32, U16 = mybir.dt.bfloat16, mybir.dt.float32, mybir.dt.uint16
+ACT = mybir.ActivationFunctionType
+MULT = mybir.AluOpType.mult
+
+
+def tile_deltatemporalmodel_kernel(tc, table, w, b, offs, out):
+    nc = tc.nc
+    with (
+        tc.tile_pool(name="held", bufs=1) as held,
+        tc.tile_pool(name="work", bufs=3) as work,
+        tc.tile_pool(name="results", bufs=4) as results,
+        tc.psum_pool(name="sums_psum", bufs=3) as sums_psum,
+        tc.psum_pool(name="proj_psum", bufs=4) as proj_psum,
+    ):
+        raw = held.tile([P, S], BF16, name="raw")
+        for c in range(S // BANK):
+            words = slice(c * BANK, (c + 1) * BANK)
+            queue = nc.sync if c % 2 == 0 else nc.scalar
+            queue.dma_start(raw[:, words], table[:, words])
+        offsets = held.tile([P, N // 16], U16, name="offsets")
+        nc.sync.dma_start(offsets[:], offs)
+        weights = held.tile([P, M], BF16, name="weights")
+        nc.scalar.dma_start(weights[:], w)
+        bias = [held.tile([P, 1], F32, name=f"bias{h}") for h in range(M // P)]
+        for h in range(M // P):
+            nc.scalar.dma_start(bias[h][:], b[h * P : (h + 1) * P, :])
+
+        ones = held.tile([P, P], F32, name="ones")
+        nc.vector.memset(ones[:], 1.0)
+
+        scaled = held.tile([P, S], BF16, name="scaled")
+        for c in range(S // BANK):
+            words = slice(c * BANK, (c + 1) * BANK)
+            squares = work.tile([P, BANK], F32, name="squares")
+            if c % 2 == 0:
+                nc.scalar.activation(squares[:], raw[:, words], ACT.Square)
+            else:
+                nc.vector.tensor_tensor(squares[:], raw[:, words], raw[:, words], MULT)
+            sums = sums_psum.tile([P, BANK], F32, name="sums")
+            nc.tensor.matmul(sums[:], ones[:], squares[:], start=True, stop=True)
+            inv_norm = work.tile([P, BANK], F32, name="inv_norm")
+            nc.scalar.activation(inv_norm[:], sums[:], ACT.Abs_reciprocal_sqrt)
+            nc.vector.tensor_tensor(scaled[:, words], raw[:, words], inv_norm[:], MULT)
+
+        for t in range(N // BANK):
+            tokens = slice(t * BANK, (t + 1) * BANK)
+            piece = offsets[:, t * (BANK // 16) : (t + 1) * (BANK // 16)]
+            for h in range(M // P):
+                units = slice(h * P, (h + 1) * P)
+                proj = proj_psum.tile([P, BANK], F32, name="proj")
+                nc.tensor.matmul(
+                    proj[:], weights[:, units], scaled[:].indirect(piece), start=True, stop=True
+                )
+                hidden = results.tile([P, BANK], F32, name="hidden")
+                nc.scalar.activation(hidden[:], proj[:], ACT.Tanh, bias=bias[h][:])
+                queue = nc.sync if h == 0 else nc.gpsimd
+                queue.dma_start(out[units, tokens], hidden[:])

@@ -3,6 +3,7 @@ import concourse.mybir as mybir
 E, S, M, N = 128, 4096, 256, 1024
 P = 128
 BANK = 512
+BANKS = 8
 FLOPS = 2 * E * M * N
 
 BF16, F32, U16 = mybir.dt.bfloat16, mybir.dt.float32, mybir.dt.uint16
@@ -12,41 +13,45 @@ MULT = mybir.AluOpType.mult
 
 def tile_deltatemporalmodel_kernel(tc, table, w, b, offs, out):
     nc = tc.nc
+    blocks = [slice(c * BANK, (c + 1) * BANK) for c in range(S // BANK)]
     with (
         tc.tile_pool(name="held", bufs=1) as held,
         tc.tile_pool(name="work", bufs=3) as work,
         tc.tile_pool(name="results", bufs=4) as results,
-        tc.psum_pool(name="sums_psum", bufs=3) as sums_psum,
-        tc.psum_pool(name="proj_psum", bufs=4) as proj_psum,
+        tc.psum_pool(name="psum", bufs=BANKS) as psum,
     ):
         raw = held.tile([P, S], BF16, name="raw")
-        for c in range(S // BANK):
-            words = slice(c * BANK, (c + 1) * BANK)
+        for c, words in enumerate(blocks):
             queue = nc.sync if c % 2 == 0 else nc.scalar
             queue.dma_start(raw[:, words], table[:, words])
         offsets = held.tile([P, N // 16], U16, name="offsets")
         nc.sync.dma_start(offsets[:], offs)
         weights = held.tile([P, M], BF16, name="weights")
-        nc.scalar.dma_start(weights[:], w)
+        nc.gpsimd.dma_start(weights[:], w)
         bias = [held.tile([P, 1], F32, name=f"bias{h}") for h in range(M // P)]
         for h in range(M // P):
-            nc.scalar.dma_start(bias[h][:], b[h * P : (h + 1) * P, :])
+            nc.gpsimd.dma_start(bias[h][:], b[h * P : (h + 1) * P, :])
 
         ones = held.tile([P, P], F32, name="ones")
         nc.vector.memset(ones[:], 1.0)
 
-        scaled = held.tile([P, S], BF16, name="scaled")
-        for c in range(S // BANK):
-            words = slice(c * BANK, (c + 1) * BANK)
-            squares = work.tile([P, BANK], F32, name="squares")
+        early = held.tile([P, 1], F32, name="early")
+        nc.scalar.activation(early[:], ones[:, 0:1], ACT.Abs_reciprocal_sqrt)
+
+        squares = held.tile([P, S], F32, name="squares")
+        sums = []
+        for c, words in enumerate(blocks):
             if c % 2 == 0:
-                nc.scalar.activation(squares[:], raw[:, words], ACT.Square)
+                nc.vector.tensor_tensor(squares[:, words], raw[:, words], raw[:, words], MULT)
             else:
-                nc.vector.tensor_tensor(squares[:], raw[:, words], raw[:, words], MULT)
-            sums = sums_psum.tile([P, BANK], F32, name="sums")
-            nc.tensor.matmul(sums[:], ones[:], squares[:], start=True, stop=True)
+                nc.scalar.activation(squares[:, words], raw[:, words], ACT.Square)
+            sums.append(psum.tile([P, BANK], F32, name=f"sums{c}", tag="bank"))
+            nc.tensor.matmul(sums[c][:], ones[:], squares[:, words], start=True, stop=True)
+
+        scaled = held.tile([P, S], BF16, name="scaled")
+        for c, words in enumerate(blocks):
             inv_norm = work.tile([P, BANK], F32, name="inv_norm")
-            nc.scalar.activation(inv_norm[:], sums[:], ACT.Abs_reciprocal_sqrt)
+            nc.scalar.activation(inv_norm[:], sums[c][:], ACT.Abs_reciprocal_sqrt)
             nc.vector.tensor_tensor(scaled[:, words], raw[:, words], inv_norm[:], MULT)
 
         for t in range(N // BANK):
@@ -54,11 +59,10 @@ def tile_deltatemporalmodel_kernel(tc, table, w, b, offs, out):
             piece = offsets[:, t * (BANK // 16) : (t + 1) * (BANK // 16)]
             for h in range(M // P):
                 units = slice(h * P, (h + 1) * P)
-                proj = proj_psum.tile([P, BANK], F32, name="proj")
+                proj = psum.tile([P, BANK], F32, name="proj", tag="bank")
                 nc.tensor.matmul(
                     proj[:], weights[:, units], scaled[:].indirect(piece), start=True, stop=True
                 )
                 hidden = results.tile([P, BANK], F32, name="hidden")
                 nc.scalar.activation(hidden[:], proj[:], ACT.Tanh, bias=bias[h][:])
-                queue = nc.sync if h == 0 else nc.gpsimd
-                queue.dma_start(out[units, tokens], hidden[:])
+                nc.sync.dma_start(out[units, tokens], hidden[:])

@@ -9,6 +9,7 @@ FLOPS = 2 * E * M * N
 BF16, F32, U16 = mybir.dt.bfloat16, mybir.dt.float32, mybir.dt.uint16
 ACT = mybir.ActivationFunctionType
 MULT = mybir.AluOpType.mult
+WARM_UP = 6
 
 
 def tile_deltatemporalmodel_kernel(tc, table, w, b, offs, out):
@@ -34,6 +35,10 @@ def tile_deltatemporalmodel_kernel(tc, table, w, b, offs, out):
 
         ones = held.tile([P, P], F32, name="ones")
         nc.vector.memset(ones[:], 1.0)
+
+        unread = psum.tile([P, BANK], F32, name="unread", tag="bank")
+        for i in range(WARM_UP):
+            nc.tensor.matmul(unread[:, 0:P], ones[:], ones[:], start=True, stop=True)
 
         early = held.tile([P, 1], F32, name="early")
         nc.scalar.activation(early[:], ones[:, 0:1], ACT.Abs_reciprocal_sqrt)

@@ -10,6 +10,7 @@ BF16, F32, U16 = mybir.dt.bfloat16, mybir.dt.float32, mybir.dt.uint16
 ACT = mybir.ActivationFunctionType
 MULT = mybir.AluOpType.mult
 WARM_UP = 6
+BRIDGE = 5
 
 
 def tile_deltatemporalmodel_kernel(tc, table, w, b, offs, out):
@@ -36,9 +37,12 @@ def tile_deltatemporalmodel_kernel(tc, table, w, b, offs, out):
         ones = held.tile([P, P], F32, name="ones")
         nc.vector.memset(ones[:], 1.0)
 
-        unread = psum.tile([P, BANK], F32, name="unread", tag="bank")
-        for i in range(WARM_UP):
-            nc.tensor.matmul(unread[:, 0:P], ones[:], ones[:], start=True, stop=True)
+        def idle_matmuls(count):
+            unread = psum.tile([P, BANK], F32, name="unread", tag="bank")
+            for i in range(count):
+                nc.tensor.matmul(unread[:, 0:P], ones[:], ones[:], start=True, stop=True)
+
+        idle_matmuls(WARM_UP)
 
         early = held.tile([P, 1], F32, name="early")
         nc.scalar.activation(early[:], ones[:, 0:1], ACT.Abs_reciprocal_sqrt)
@@ -52,6 +56,8 @@ def tile_deltatemporalmodel_kernel(tc, table, w, b, offs, out):
                 nc.scalar.activation(squares[:, words], raw[:, words], ACT.Square)
             sums.append(psum.tile([P, BANK], F32, name=f"sums{c}", tag="bank"))
             nc.tensor.matmul(sums[c][:], ones[:], squares[:, words], start=True, stop=True)
+
+        idle_matmuls(BRIDGE)
 
         scaled = held.tile([P, S], BF16, name="scaled")
         for c, words in enumerate(blocks):

@@ -4,18 +4,19 @@ E, S, M, N = 128, 4096, 256, 1024
 P = 128
 BANK = 512
 BANKS = 8
+WIDTHS = (BANK // 4, BANK // 4, BANK // 2) + (BANK,) * 6 + (BANK // 2, BANK // 4, BANK // 4)
+assert sum(WIDTHS) == S and max(WIDTHS) <= BANK
 FLOPS = 2 * E * M * N
 
 BF16, F32, U16 = mybir.dt.bfloat16, mybir.dt.float32, mybir.dt.uint16
 ACT = mybir.ActivationFunctionType
 MULT = mybir.AluOpType.mult
 WARM_UP = 6
-BRIDGE = 5
 
 
 def tile_deltatemporalmodel_kernel(tc, table, w, b, offs, out):
     nc = tc.nc
-    blocks = [slice(c * BANK, (c + 1) * BANK) for c in range(S // BANK)]
+    blocks = [slice(sum(WIDTHS[:c]), sum(WIDTHS[: c + 1])) for c in range(len(WIDTHS))]
     with (
         tc.tile_pool(name="held", bufs=1) as held,
         tc.tile_pool(name="work", bufs=3) as work,
@@ -37,12 +38,9 @@ def tile_deltatemporalmodel_kernel(tc, table, w, b, offs, out):
         ones = held.tile([P, P], F32, name="ones")
         nc.vector.memset(ones[:], 1.0)
 
-        def idle_matmuls(count):
-            unread = psum.tile([P, BANK], F32, name="unread", tag="bank")
-            for i in range(count):
-                nc.tensor.matmul(unread[:, 0:P], ones[:], ones[:], start=True, stop=True)
-
-        idle_matmuls(WARM_UP)
+        unread = psum.tile([P, BANK], F32, name="unread", tag="bank")
+        for i in range(WARM_UP):
+            nc.tensor.matmul(unread[:, 0:P], ones[:], ones[:], start=True, stop=True)
 
         early = held.tile([P, 1], F32, name="early")
         nc.scalar.activation(early[:], ones[:, 0:1], ACT.Abs_reciprocal_sqrt)
@@ -55,15 +53,16 @@ def tile_deltatemporalmodel_kernel(tc, table, w, b, offs, out):
             else:
                 nc.scalar.activation(squares[:, words], raw[:, words], ACT.Square)
             sums.append(psum.tile([P, BANK], F32, name=f"sums{c}", tag="bank"))
-            nc.tensor.matmul(sums[c][:], ones[:], squares[:, words], start=True, stop=True)
-
-        idle_matmuls(BRIDGE)
+            nc.tensor.matmul(
+                sums[c][:, 0 : WIDTHS[c]], ones[:], squares[:, words], start=True, stop=True
+            )
 
         scaled = held.tile([P, S], BF16, name="scaled")
         for c, words in enumerate(blocks):
             inv_norm = work.tile([P, BANK], F32, name="inv_norm")
-            nc.scalar.activation(inv_norm[:], sums[c][:], ACT.Abs_reciprocal_sqrt)
-            nc.vector.tensor_tensor(scaled[:, words], raw[:, words], inv_norm[:], MULT)
+            width = WIDTHS[c]
+            nc.scalar.activation(inv_norm[:, 0:width], sums[c][:, 0:width], ACT.Abs_reciprocal_sqrt)
+            nc.vector.tensor_tensor(scaled[:, words], raw[:, words], inv_norm[:, 0:width], MULT)
 
         for t in range(N // BANK):
             tokens = slice(t * BANK, (t + 1) * BANK)

@@ -4,7 +4,7 @@ E, S, M, N = 128, 4096, 256, 1024
 P = 128
 BANK = 512
 BANKS = 8
-WIDTHS = (BANK // 4, BANK // 4, BANK // 2) + (BANK,) * 6 + (BANK // 2, BANK // 4, BANK // 4)
+WIDTHS = (BANK,) * 7 + (BANK // 2, BANK // 4, BANK // 4)
 assert sum(WIDTHS) == S and max(WIDTHS) <= BANK
 FLOPS = 2 * E * M * N
 
@@ -16,6 +16,7 @@ WARM_UP = 6
 
 def tile_deltatemporalmodel_kernel(tc, table, w, b, offs, out):
     nc = tc.nc
+    loads = [slice(c * BANK, (c + 1) * BANK) for c in range(S // BANK)]
     blocks = [slice(sum(WIDTHS[:c]), sum(WIDTHS[: c + 1])) for c in range(len(WIDTHS))]
     with (
         tc.tile_pool(name="held", bufs=1) as held,
@@ -24,7 +25,7 @@ def tile_deltatemporalmodel_kernel(tc, table, w, b, offs, out):
         tc.psum_pool(name="psum", bufs=BANKS) as psum,
     ):
         raw = held.tile([P, S], BF16, name="raw")
-        for c, words in enumerate(blocks):
+        for c, words in enumerate(loads):
             queue = nc.sync if c % 2 == 0 else nc.scalar
             queue.dma_start(raw[:, words], table[:, words])
         offsets = held.tile([P, N // 16], U16, name="offsets")

@@ -4,8 +4,6 @@ E, S, M, N = 128, 4096, 256, 1024
 P = 128
 BANK = 512
 BANKS = 8
-WIDTHS = (BANK,) * 7 + (BANK // 2, BANK // 4, BANK // 4)
-assert sum(WIDTHS) == S and max(WIDTHS) <= BANK
 FLOPS = 2 * E * M * N
 
 BF16, F32, U16 = mybir.dt.bfloat16, mybir.dt.float32, mybir.dt.uint16
@@ -16,8 +14,7 @@ WARM_UP = 6
 
 def tile_deltatemporalmodel_kernel(tc, table, w, b, offs, out):
     nc = tc.nc
-    loads = [slice(c * BANK, (c + 1) * BANK) for c in range(S // BANK)]
-    blocks = [slice(sum(WIDTHS[:c]), sum(WIDTHS[: c + 1])) for c in range(len(WIDTHS))]
+    blocks = [slice(c * BANK, (c + 1) * BANK) for c in range(S // BANK)]
     with (
         tc.tile_pool(name="held", bufs=1) as held,
         tc.tile_pool(name="work", bufs=3) as work,
@@ -25,9 +22,8 @@ def tile_deltatemporalmodel_kernel(tc, table, w, b, offs, out):
         tc.psum_pool(name="psum", bufs=BANKS) as psum,
     ):
         raw = held.tile([P, S], BF16, name="raw")
-        for c, words in enumerate(loads):
-            queue = nc.sync if c % 2 == 0 else nc.scalar
-            queue.dma_start(raw[:, words], table[:, words])
+        for c, words in enumerate(blocks):
+            nc.sync.dma_start(raw[:, words], table[:, words])
         offsets = held.tile([P, N // 16], U16, name="offsets")
         nc.sync.dma_start(offsets[:], offs)
         weights = held.tile([P, M], BF16, name="weights")
@@ -54,16 +50,13 @@ def tile_deltatemporalmodel_kernel(tc, table, w, b, offs, out):
             else:
                 nc.scalar.activation(squares[:, words], raw[:, words], ACT.Square)
             sums.append(psum.tile([P, BANK], F32, name=f"sums{c}", tag="bank"))
-            nc.tensor.matmul(
-                sums[c][:, 0 : WIDTHS[c]], ones[:], squares[:, words], start=True, stop=True
-            )
+            nc.tensor.matmul(sums[c][:], ones[:], squares[:, words], start=True, stop=True)
 
         scaled = held.tile([P, S], BF16, name="scaled")
         for c, words in enumerate(blocks):
             inv_norm = work.tile([P, BANK], F32, name="inv_norm")
-            width = WIDTHS[c]
-            nc.scalar.activation(inv_norm[:, 0:width], sums[c][:, 0:width], ACT.Abs_reciprocal_sqrt)
-            nc.vector.tensor_tensor(scaled[:, words], raw[:, words], inv_norm[:, 0:width], MULT)
+            nc.scalar.activation(inv_norm[:], sums[c][:], ACT.Abs_reciprocal_sqrt)
+            nc.vector.tensor_tensor(scaled[:, words], raw[:, words], inv_norm[:], MULT)
 
         for t in range(N // BANK):
             tokens = slice(t * BANK, (t + 1) * BANK)

@@ -8,7 +8,7 @@ FLOPS = 2 * E * M * N
 
 BF16, F32, U16 = mybir.dt.bfloat16, mybir.dt.float32, mybir.dt.uint16
 ACT = mybir.ActivationFunctionType
-MULT = mybir.AluOpType.mult
+MULT, SUBTRACT = mybir.AluOpType.mult, mybir.AluOpType.subtract
 WARM_UP = 6
 
 
@@ -34,6 +34,8 @@ def tile_deltatemporalmodel_kernel(tc, table, w, b, offs, out):
 
         ones = held.tile([P, P], F32, name="ones")
         nc.vector.memset(ones[:], 1.0)
+        ones_bf16 = held.tile([P, P], BF16, name="ones_bf16")
+        nc.vector.memset(ones_bf16[:], 1.0)
 
         unread = psum.tile([P, BANK], F32, name="unread", tag="bank")
         for i in range(WARM_UP):
@@ -45,12 +47,20 @@ def tile_deltatemporalmodel_kernel(tc, table, w, b, offs, out):
         squares = held.tile([P, S], F32, name="squares")
         sums = []
         for c, words in enumerate(blocks):
-            if c % 2 == 0:
+            if c % 4 == 0:
                 nc.vector.tensor_tensor(squares[:, words], raw[:, words], raw[:, words], MULT)
             else:
                 nc.scalar.activation(squares[:, words], raw[:, words], ACT.Square)
             sums.append(psum.tile([P, BANK], F32, name=f"sums{c}", tag="bank"))
-            nc.tensor.matmul(sums[c][:], ones[:], squares[:, words], start=True, stop=True)
+            if c % 3 == 2:
+                top = work.tile([P, BANK], BF16, name="top")
+                nc.vector.tensor_tensor(top[:], raw[:, words], raw[:, words], MULT)
+                rest = work.tile([P, BANK], BF16, name="rest")
+                nc.vector.tensor_tensor(rest[:], squares[:, words], top[:], SUBTRACT)
+                nc.tensor.matmul(sums[c][:], ones_bf16[:], top[:], start=True, stop=False)
+                nc.tensor.matmul(sums[c][:], ones_bf16[:], rest[:], start=False, stop=True)
+            else:
+                nc.tensor.matmul(sums[c][:], ones[:], squares[:, words], start=True, stop=True)
 
         scaled = held.tile([P, S], BF16, name="scaled")
         for c, words in enumerate(blocks):

@@ -22,8 +22,11 @@ def tile_deltatemporalmodel_kernel(tc, table, w, b, offs, out):
         tc.psum_pool(name="psum", bufs=BANKS) as psum,
     ):
         raw = held.tile([P, S], BF16, name="raw")
-        for c, words in enumerate(blocks):
-            nc.sync.dma_start(raw[:, words], table[:, words])
+        first_word = 0
+        for blocks_in_piece in (1, 1, 2, 2, 2):
+            piece = slice(first_word, first_word + blocks_in_piece * BANK)
+            nc.sync.dma_start(raw[:, piece], table[:, piece])
+            first_word = piece.stop
         offsets = held.tile([P, N // 16], U16, name="offsets")
         nc.sync.dma_start(offsets[:], offs)
         weights = held.tile([P, M], BF16, name="weights")
@@ -47,17 +50,16 @@ def tile_deltatemporalmodel_kernel(tc, table, w, b, offs, out):
         squares = held.tile([P, S], F32, name="squares")
         sums = []
         for c, words in enumerate(blocks):
-            if c % 4 == 0:
+            if c % 2 == 0:
                 nc.vector.tensor_tensor(squares[:, words], raw[:, words], raw[:, words], MULT)
             else:
                 nc.scalar.activation(squares[:, words], raw[:, words], ACT.Square)
             sums.append(psum.tile([P, BANK], F32, name=f"sums{c}", tag="bank"))
-            if c % 3 == 2:
-                top = work.tile([P, BANK], BF16, name="top")
-                nc.vector.tensor_tensor(top[:], raw[:, words], raw[:, words], MULT)
+            if c % 2 == 1:
+                top = squares[:, words].bitcast(BF16)[:, 1::2]
                 rest = work.tile([P, BANK], BF16, name="rest")
-                nc.vector.tensor_tensor(rest[:], squares[:, words], top[:], SUBTRACT)
-                nc.tensor.matmul(sums[c][:], ones_bf16[:], top[:], start=True, stop=False)
+                nc.vector.tensor_tensor(rest[:], squares[:, words], top, SUBTRACT)
+                nc.tensor.matmul(sums[c][:], ones_bf16[:], top, start=True, stop=False)
                 nc.tensor.matmul(sums[c][:], ones_bf16[:], rest[:], start=False, stop=True)
             else:
                 nc.tensor.matmul(sums[c][:], ones[:], squares[:, words], start=True, stop=True)

@@ -17,7 +17,7 @@ def tile_deltatemporalmodel_kernel(tc, table, w, b, offs, out):
     blocks = [slice(c * BANK, (c + 1) * BANK) for c in range(S // BANK)]
     with (
         tc.tile_pool(name="held", bufs=1) as held,
-        tc.tile_pool(name="work", bufs=3) as work,
+        tc.tile_pool(name="work", bufs=8) as work,
         tc.tile_pool(name="results", bufs=4) as results,
         tc.psum_pool(name="psum", bufs=BANKS) as psum,
     ):
@@ -50,12 +50,12 @@ def tile_deltatemporalmodel_kernel(tc, table, w, b, offs, out):
         squares = held.tile([P, S], F32, name="squares")
         sums = []
         for c, words in enumerate(blocks):
-            if c % 2 == 0:
+            if c % 4 == 0:
                 nc.vector.tensor_tensor(squares[:, words], raw[:, words], raw[:, words], MULT)
             else:
                 nc.scalar.activation(squares[:, words], raw[:, words], ACT.Square)
             sums.append(psum.tile([P, BANK], F32, name=f"sums{c}", tag="bank"))
-            if c % 2 == 1:
+            if c % 4 != 0:
                 top = squares[:, words].bitcast(BF16)[:, 1::2]
                 rest = work.tile([P, BANK], BF16, name="rest")
                 nc.vector.tensor_tensor(rest[:], squares[:, words], top, SUBTRACT)

@@ -30,10 +30,9 @@ def tile_deltatemporalmodel_kernel(tc, table, w, b, offs, out):
         offsets = held.tile([P, N // 16], U16, name="offsets")
         nc.sync.dma_start(offsets[:], offs)
         weights = held.tile([P, M], BF16, name="weights")
-        nc.gpsimd.dma_start(weights[:], w)
-        bias = [held.tile([P, 1], F32, name=f"bias{h}") for h in range(M // P)]
-        for h in range(M // P):
-            nc.gpsimd.dma_start(bias[h][:], b[h * P : (h + 1) * P, :])
+        nc.sync.dma_start(weights[:], w)
+        bias = held.tile([P, M // P], F32, name="bias")
+        nc.sync.dma_start(bias[:], b.rearrange("(h p) one -> p (h one)", p=P))
 
         ones = held.tile([P, P], F32, name="ones")
         nc.vector.memset(ones[:], 1.0)
@@ -80,5 +79,5 @@ def tile_deltatemporalmodel_kernel(tc, table, w, b, offs, out):
                     proj[:], weights[:, units], scaled[:].indirect(piece), start=True, stop=True
                 )
                 hidden = results.tile([P, BANK], F32, name="hidden")
-                nc.scalar.activation(hidden[:], proj[:], ACT.Tanh, bias=bias[h][:])
+                nc.scalar.activation(hidden[:], proj[:], ACT.Tanh, bias=bias[:, h : h + 1])
                 nc.sync.dma_start(out[units, tokens], hidden[:])

@@ -9,7 +9,7 @@ FLOPS = 2 * E * M * N
 BF16, F32, U16 = mybir.dt.bfloat16, mybir.dt.float32, mybir.dt.uint16
 ACT = mybir.ActivationFunctionType
 MULT, SUBTRACT = mybir.AluOpType.mult, mybir.AluOpType.subtract
-WARM_UP = 6
+WARM_UP = 4
 
 
 def tile_deltatemporalmodel_kernel(tc, table, w, b, offs, out):

@@ -54,7 +54,7 @@ def tile_deltatemporalmodel_kernel(tc, table, w, b, offs, out):
             else:
                 nc.scalar.activation(squares[:, words], raw[:, words], ACT.Square)
             sums.append(psum.tile([P, BANK], F32, name=f"sums{c}", tag="bank"))
-            if c % 4 != 0:
+            if c % 4 != 0 and c != len(blocks) - 1:
                 top = squares[:, words].bitcast(BF16)[:, 1::2]
                 rest = work.tile([P, BANK], BF16, name="rest")
                 nc.vector.tensor_tensor(rest[:], squares[:, words], top, SUBTRACT)

@@ -49,12 +49,12 @@ def tile_deltatemporalmodel_kernel(tc, table, w, b, offs, out):
         squares = held.tile([P, S], F32, name="squares")
         sums = []
         for c, words in enumerate(blocks):
-            if c % 4 == 0:
+            if c % 4 == 1:
                 nc.vector.tensor_tensor(squares[:, words], raw[:, words], raw[:, words], MULT)
             else:
                 nc.scalar.activation(squares[:, words], raw[:, words], ACT.Square)
             sums.append(psum.tile([P, BANK], F32, name=f"sums{c}", tag="bank"))
-            if c % 4 != 0 and c != len(blocks) - 1:
+            if c % 4 != 1 and c != len(blocks) - 1:
                 top = squares[:, words].bitcast(BF16)[:, 1::2]
                 rest = work.tile([P, BANK], BF16, name="rest")
                 nc.vector.tensor_tensor(rest[:], squares[:, words], top, SUBTRACT)

@@ -1,32 +1,33 @@
 import concourse.mybir as mybir
+from concourse.masks import make_identity
 
 E, S, M, N = 128, 4096, 256, 1024
 P = 128
 BANK = 512
 BANKS = 8
+QUAD = 32
+UNIT = 1024
+GROUPS = UNIT // P
 FLOPS = 2 * E * M * N
 
 BF16, F32, U16 = mybir.dt.bfloat16, mybir.dt.float32, mybir.dt.uint16
 ACT = mybir.ActivationFunctionType
-MULT, SUBTRACT = mybir.AluOpType.mult, mybir.AluOpType.subtract
+ADD, MULT, MAX = mybir.AluOpType.add, mybir.AluOpType.mult, mybir.AluOpType.max
+X = mybir.AxisListType.X
+FAR_BELOW = 2.0**127
 WARM_UP = 4
 
 
 def tile_deltatemporalmodel_kernel(tc, table, w, b, offs, out):
     nc = tc.nc
-    blocks = [slice(c * BANK, (c + 1) * BANK) for c in range(S // BANK)]
     with (
         tc.tile_pool(name="held", bufs=1) as held,
-        tc.tile_pool(name="work", bufs=8) as work,
         tc.tile_pool(name="results", bufs=4) as results,
         tc.psum_pool(name="psum", bufs=BANKS) as psum,
     ):
         raw = held.tile([P, S], BF16, name="raw")
-        first_word = 0
-        for blocks_in_piece in (1, 1, 2, 2, 2):
-            piece = slice(first_word, first_word + blocks_in_piece * BANK)
-            nc.sync.dma_start(raw[:, piece], table[:, piece])
-            first_word = piece.stop
+        for first in range(0, S, UNIT):
+            nc.sync.dma_start(raw[:, first : first + UNIT], table[:, first : first + UNIT])
         offsets = held.tile([P, N // 16], U16, name="offsets")
         nc.sync.dma_start(offsets[:], offs)
         weights = held.tile([P, M], BF16, name="weights")
@@ -36,38 +37,64 @@ def tile_deltatemporalmodel_kernel(tc, table, w, b, offs, out):
 
         ones = held.tile([P, P], F32, name="ones")
         nc.vector.memset(ones[:], 1.0)
-        ones_bf16 = held.tile([P, P], BF16, name="ones_bf16")
-        nc.vector.memset(ones_bf16[:], 1.0)
+        early = held.tile([P, 1], F32, name="early")
+        nc.scalar.activation(early[:], ones[:, 0:1], ACT.Abs_reciprocal_sqrt)
 
         unread = psum.tile([P, BANK], F32, name="unread", tag="bank")
         for i in range(WARM_UP):
             nc.tensor.matmul(unread[:, 0:P], ones[:], ones[:], start=True, stop=True)
 
-        early = held.tile([P, 1], F32, name="early")
-        nc.scalar.activation(early[:], ones[:, 0:1], ACT.Abs_reciprocal_sqrt)
+        identity = held.tile([P, P], F32, name="identity")
+        make_identity(nc, identity[:])
+        identity_bf16 = held.tile([P, P], BF16, name="identity_bf16")
+        nc.vector.tensor_copy(identity_bf16[:], identity[:])
+        pairs = held.tile([P, 2 * QUAD], F32, name="pairs")
+        nc.vector.tensor_tensor(
+            pairs[:], identity[:, 0 : 2 * QUAD], identity[:, 2 * QUAD : 4 * QUAD], ADD
+        )
+        own = held.tile([P, QUAD], F32, name="own")
+        nc.vector.tensor_tensor(own[:], pairs[:, 0:QUAD], pairs[:, QUAD : 2 * QUAD], ADD)
+        mask = held.tile([P, GROUPS, QUAD], BF16, name="mask")
+        nc.vector.tensor_scalar(
+            mask[:], own[:].unsqueeze(1).to_broadcast([P, GROUPS, QUAD]), -1.0, FAR_BELOW, ADD, MULT
+        )
 
-        squares = held.tile([P, S], F32, name="squares")
-        sums = []
-        for c, words in enumerate(blocks):
-            if c % 4 == 1:
-                nc.vector.tensor_tensor(squares[:, words], raw[:, words], raw[:, words], MULT)
-            else:
-                nc.scalar.activation(squares[:, words], raw[:, words], ACT.Square)
-            sums.append(psum.tile([P, BANK], F32, name=f"sums{c}", tag="bank"))
-            if c % 4 != 1 and c != len(blocks) - 1:
-                top = squares[:, words].bitcast(BF16)[:, 1::2]
-                rest = work.tile([P, BANK], BF16, name="rest")
-                nc.vector.tensor_tensor(rest[:], squares[:, words], top, SUBTRACT)
-                nc.tensor.matmul(sums[c][:], ones_bf16[:], top, start=True, stop=False)
-                nc.tensor.matmul(sums[c][:], ones_bf16[:], rest[:], start=False, stop=True)
-            else:
-                nc.tensor.matmul(sums[c][:], ones[:], squares[:, words], start=True, stop=True)
-
+        lengths = held.tile([P, S // P], F32, name="lengths")
+        inv = held.tile([P, S // P], F32, name="inv")
         scaled = held.tile([P, S], BF16, name="scaled")
-        for c, words in enumerate(blocks):
-            inv_norm = work.tile([P, BANK], F32, name="inv_norm")
-            nc.scalar.activation(inv_norm[:], sums[c][:], ACT.Abs_reciprocal_sqrt)
-            nc.vector.tensor_tensor(scaled[:, words], raw[:, words], inv_norm[:], MULT)
+        for u in range(S // UNIT + 1):
+            if u < S // UNIT:
+                gram = psum.tile([P, BANK], F32, name="gram", tag="bank")
+                masked = gram[:, 0 : GROUPS * QUAD]
+                nc.tensor.matmul(
+                    masked, identity_bf16[:], mask[:].rearrange("p g n -> p (g n)"),
+                    start=True, stop=False,
+                )
+                for g in range(GROUPS):
+                    for q in range(P // QUAD):
+                        first = u * UNIT + g * P + q * QUAD
+                        words = raw[:, first : first + QUAD]
+                        nc.tensor.matmul(
+                            gram[q * QUAD : (q + 1) * QUAD, g * QUAD : (g + 1) * QUAD],
+                            words, words, start=False, stop=g == GROUPS - 1,
+                        )
+                unit = slice(u * GROUPS, (u + 1) * GROUPS)
+                nc.vector.tensor_reduce(
+                    lengths[:, unit], masked.rearrange("p (g n) -> p g n", n=QUAD), X, MAX
+                )
+                nc.scalar.activation(inv[:, unit], lengths[:, unit], ACT.Abs_reciprocal_sqrt)
+            if u > 0:
+                for first in range((u - 1) * UNIT, u * UNIT, BANK):
+                    spread = psum.tile([P, BANK], F32, name="spread", tag="bank")
+                    for g in range(BANK // P):
+                        column = first // P + g
+                        nc.tensor.transpose(
+                            spread[:, g * P : (g + 1) * P],
+                            inv[:, column : column + 1].to_broadcast([P, P]),
+                            identity[:],
+                        )
+                    words = slice(first, first + BANK)
+                    nc.vector.tensor_tensor(scaled[:, words], raw[:, words], spread[:], MULT)
 
         for t in range(N // BANK):
             tokens = slice(t * BANK, (t + 1) * BANK)

@@ -6,8 +6,8 @@ P = 128
 BANK = 512
 BANKS = 8
 QUAD = 32
-UNIT = 1024
-GROUPS = UNIT // P
+UNITS = (512, 1024, 1024, 1024, 512)
+WIDEST = max(UNITS) // P
 FLOPS = 2 * E * M * N
 
 BF16, F32, U16 = mybir.dt.bfloat16, mybir.dt.float32, mybir.dt.uint16
@@ -15,19 +15,20 @@ ACT = mybir.ActivationFunctionType
 ADD, MULT, MAX = mybir.AluOpType.add, mybir.AluOpType.mult, mybir.AluOpType.max
 X = mybir.AxisListType.X
 FAR_BELOW = 2.0**127
-WARM_UP = 4
+WARM_UP = 3
 
 
 def tile_deltatemporalmodel_kernel(tc, table, w, b, offs, out):
     nc = tc.nc
+    units = [slice(sum(UNITS[:u]), sum(UNITS[: u + 1])) for u in range(len(UNITS))]
     with (
         tc.tile_pool(name="held", bufs=1) as held,
         tc.tile_pool(name="results", bufs=4) as results,
         tc.psum_pool(name="psum", bufs=BANKS) as psum,
     ):
         raw = held.tile([P, S], BF16, name="raw")
-        for first in range(0, S, UNIT):
-            nc.sync.dma_start(raw[:, first : first + UNIT], table[:, first : first + UNIT])
+        for words in units:
+            nc.sync.dma_start(raw[:, words], table[:, words])
         offsets = held.tile([P, N // 16], U16, name="offsets")
         nc.sync.dma_start(offsets[:], offs)
         weights = held.tile([P, M], BF16, name="weights")
@@ -54,47 +55,55 @@ def tile_deltatemporalmodel_kernel(tc, table, w, b, offs, out):
         )
         own = held.tile([P, QUAD], F32, name="own")
         nc.vector.tensor_tensor(own[:], pairs[:, 0:QUAD], pairs[:, QUAD : 2 * QUAD], ADD)
-        mask = held.tile([P, GROUPS, QUAD], BF16, name="mask")
+        mask = held.tile([P, WIDEST * QUAD], BF16, name="mask")
         nc.vector.tensor_scalar(
-            mask[:], own[:].unsqueeze(1).to_broadcast([P, GROUPS, QUAD]), -1.0, FAR_BELOW, ADD, MULT
+            mask[:].rearrange("p (g n) -> p g n", n=QUAD),
+            own[:].unsqueeze(1).to_broadcast([P, WIDEST, QUAD]),
+            -1.0, FAR_BELOW, ADD, MULT,
         )
 
         lengths = held.tile([P, S // P], F32, name="lengths")
         inv = held.tile([P, S // P], F32, name="inv")
         scaled = held.tile([P, S], BF16, name="scaled")
-        for u in range(S // UNIT + 1):
-            if u < S // UNIT:
-                gram = psum.tile([P, BANK], F32, name="gram", tag="bank")
-                masked = gram[:, 0 : GROUPS * QUAD]
-                nc.tensor.matmul(
-                    masked, identity_bf16[:], mask[:].rearrange("p g n -> p (g n)"),
-                    start=True, stop=False,
-                )
-                for g in range(GROUPS):
-                    for q in range(P // QUAD):
-                        first = u * UNIT + g * P + q * QUAD
-                        words = raw[:, first : first + QUAD]
-                        nc.tensor.matmul(
-                            gram[q * QUAD : (q + 1) * QUAD, g * QUAD : (g + 1) * QUAD],
-                            words, words, start=False, stop=g == GROUPS - 1,
-                        )
-                unit = slice(u * GROUPS, (u + 1) * GROUPS)
-                nc.vector.tensor_reduce(
-                    lengths[:, unit], masked.rearrange("p (g n) -> p g n", n=QUAD), X, MAX
-                )
-                nc.scalar.activation(inv[:, unit], lengths[:, unit], ACT.Abs_reciprocal_sqrt)
-            if u > 0:
-                for first in range((u - 1) * UNIT, u * UNIT, BANK):
-                    spread = psum.tile([P, BANK], F32, name="spread", tag="bank")
-                    for g in range(BANK // P):
-                        column = first // P + g
-                        nc.tensor.transpose(
-                            spread[:, g * P : (g + 1) * P],
-                            inv[:, column : column + 1].to_broadcast([P, P]),
-                            identity[:],
-                        )
-                    words = slice(first, first + BANK)
-                    nc.vector.tensor_tensor(scaled[:, words], raw[:, words], spread[:], MULT)
+
+        def measure(unit):
+            groups = range(unit.start // P, unit.stop // P)
+            gram = psum.tile([P, BANK], F32, name="gram", tag="bank")
+            masked = gram[:, 0 : len(groups) * QUAD]
+            nc.tensor.matmul(
+                masked, identity_bf16[:], mask[:, 0 : len(groups) * QUAD], start=True, stop=False
+            )
+            for place, g in enumerate(groups):
+                for q in range(P // QUAD):
+                    words = raw[:, g * P + q * QUAD : g * P + (q + 1) * QUAD]
+                    nc.tensor.matmul(
+                        gram[q * QUAD : (q + 1) * QUAD, place * QUAD : (place + 1) * QUAD],
+                        words, words, start=False, stop=place == len(groups) - 1,
+                    )
+            columns = slice(groups.start, groups.stop)
+            nc.vector.tensor_reduce(
+                lengths[:, columns], masked.rearrange("p (g n) -> p g n", n=QUAD), X, MAX
+            )
+            nc.scalar.activation(inv[:, columns], lengths[:, columns], ACT.Abs_reciprocal_sqrt)
+
+        def scale(unit):
+            for first in range(unit.start, unit.stop, BANK):
+                spread = psum.tile([P, BANK], F32, name="spread", tag="bank")
+                for place in range(BANK // P):
+                    g = first // P + place
+                    nc.tensor.transpose(
+                        spread[:, place * P : (place + 1) * P],
+                        inv[:, g : g + 1].to_broadcast([P, P]),
+                        identity[:],
+                    )
+                words = slice(first, first + BANK)
+                nc.vector.tensor_tensor(scaled[:, words], raw[:, words], spread[:], MULT)
+
+        measure(units[0])
+        for u in range(1, len(units)):
+            measure(units[u])
+            scale(units[u - 1])
+        scale(units[-1])
 
         for t in range(N // BANK):
             tokens = slice(t * BANK, (t + 1) * BANK)

@@ -99,11 +99,10 @@ def tile_deltatemporalmodel_kernel(tc, table, w, b, offs, out):
                 words = slice(first, first + BANK)
                 nc.vector.tensor_tensor(scaled[:, words], raw[:, words], spread[:], MULT)
 
-        measure(units[0])
-        for u in range(1, len(units)):
-            measure(units[u])
-            scale(units[u - 1])
-        scale(units[-1])
+        for unit in units:
+            measure(unit)
+        for unit in units:
+            scale(unit)
 
         for t in range(N // BANK):
             tokens = slice(t * BANK, (t + 1) * BANK)

@@ -8,13 +8,13 @@ BANKS = 8
 QUAD = 32
 UNITS = (512, 1024, 1024, 1024, 512)
 WIDEST = max(UNITS) // P
+GPSIMD_BLOCKS = (1, 3)
 FLOPS = 2 * E * M * N
 
 BF16, F32, U16 = mybir.dt.bfloat16, mybir.dt.float32, mybir.dt.uint16
 ACT = mybir.ActivationFunctionType
-ADD, MULT, MAX = mybir.AluOpType.add, mybir.AluOpType.mult, mybir.AluOpType.max
+ADD, MULT = mybir.AluOpType.add, mybir.AluOpType.mult
 X = mybir.AxisListType.X
-FAR_BELOW = 2.0**127
 WARM_UP = 3
 
 
@@ -23,6 +23,7 @@ def tile_deltatemporalmodel_kernel(tc, table, w, b, offs, out):
     units = [slice(sum(UNITS[:u]), sum(UNITS[: u + 1])) for u in range(len(UNITS))]
     with (
         tc.tile_pool(name="held", bufs=1) as held,
+        tc.tile_pool(name="work", bufs=2) as work,
         tc.tile_pool(name="results", bufs=4) as results,
         tc.psum_pool(name="psum", bufs=BANKS) as psum,
     ):
@@ -47,20 +48,12 @@ def tile_deltatemporalmodel_kernel(tc, table, w, b, offs, out):
 
         identity = held.tile([P, P], F32, name="identity")
         make_identity(nc, identity[:])
-        identity_bf16 = held.tile([P, P], BF16, name="identity_bf16")
-        nc.vector.tensor_copy(identity_bf16[:], identity[:])
         pairs = held.tile([P, 2 * QUAD], F32, name="pairs")
         nc.vector.tensor_tensor(
             pairs[:], identity[:, 0 : 2 * QUAD], identity[:, 2 * QUAD : 4 * QUAD], ADD
         )
         own = held.tile([P, QUAD], F32, name="own")
         nc.vector.tensor_tensor(own[:], pairs[:, 0:QUAD], pairs[:, QUAD : 2 * QUAD], ADD)
-        mask = held.tile([P, WIDEST * QUAD], BF16, name="mask")
-        nc.vector.tensor_scalar(
-            mask[:].rearrange("p (g n) -> p g n", n=QUAD),
-            own[:].unsqueeze(1).to_broadcast([P, WIDEST, QUAD]),
-            -1.0, FAR_BELOW, ADD, MULT,
-        )
 
         lengths = held.tile([P, S // P], F32, name="lengths")
         inv = held.tile([P, S // P], F32, name="inv")
@@ -68,22 +61,23 @@ def tile_deltatemporalmodel_kernel(tc, table, w, b, offs, out):
 
         def measure(unit):
             groups = range(unit.start // P, unit.stop // P)
-            gram = psum.tile([P, BANK], F32, name="gram", tag="bank")
-            masked = gram[:, 0 : len(groups) * QUAD]
-            nc.tensor.matmul(
-                masked, identity_bf16[:], mask[:, 0 : len(groups) * QUAD], start=True, stop=False
-            )
+            gram = psum.tile([P, BANK // QUAD, QUAD], F32, name="gram", tag="bank")
             for place, g in enumerate(groups):
                 for q in range(P // QUAD):
                     words = raw[:, g * P + q * QUAD : g * P + (q + 1) * QUAD]
                     nc.tensor.matmul(
-                        gram[q * QUAD : (q + 1) * QUAD, place * QUAD : (place + 1) * QUAD],
-                        words, words, start=False, stop=place == len(groups) - 1,
+                        gram[q * QUAD : (q + 1) * QUAD, place, :], words, words, start=True, stop=True
                     )
-            columns = slice(groups.start, groups.stop)
-            nc.vector.tensor_reduce(
-                lengths[:, columns], masked.rearrange("p (g n) -> p g n", n=QUAD), X, MAX
+            picked = work.tile([P, WIDEST, QUAD], F32, name="picked")
+            diagonal = picked[:, 0 : len(groups), :]
+            nc.vector.tensor_tensor(
+                diagonal,
+                gram[:, 0 : len(groups), :],
+                own[:].unsqueeze(1).to_broadcast([P, len(groups), QUAD]),
+                MULT,
             )
+            columns = slice(groups.start, groups.stop)
+            nc.vector.tensor_reduce(lengths[:, columns], diagonal, X, ADD)
             nc.scalar.activation(inv[:, columns], lengths[:, columns], ACT.Abs_reciprocal_sqrt)
 
         def scale(unit):
@@ -97,7 +91,12 @@ def tile_deltatemporalmodel_kernel(tc, table, w, b, offs, out):
                         identity[:],
                     )
                 words = slice(first, first + BANK)
-                nc.vector.tensor_tensor(scaled[:, words], raw[:, words], spread[:], MULT)
+                if first // BANK in GPSIMD_BLOCKS:
+                    copied = work.tile([P, BANK], F32, name="copied")
+                    nc.scalar.copy(copied[:], spread[:])
+                    nc.gpsimd.tensor_tensor(scaled[:, words], raw[:, words], copied[:], MULT)
+                else:
+                    nc.vector.tensor_tensor(scaled[:, words], raw[:, words], spread[:], MULT)
 
         for unit in units:
             measure(unit)
@@ -108,11 +107,11 @@ def tile_deltatemporalmodel_kernel(tc, table, w, b, offs, out):
             tokens = slice(t * BANK, (t + 1) * BANK)
             piece = offsets[:, t * (BANK // 16) : (t + 1) * (BANK // 16)]
             for h in range(M // P):
-                units = slice(h * P, (h + 1) * P)
+                rows = slice(h * P, (h + 1) * P)
                 proj = psum.tile([P, BANK], F32, name="proj", tag="bank")
                 nc.tensor.matmul(
-                    proj[:], weights[:, units], scaled[:].indirect(piece), start=True, stop=True
+                    proj[:], weights[:, rows], scaled[:].indirect(piece), start=True, stop=True
                 )
                 hidden = results.tile([P, BANK], F32, name="hidden")
                 nc.scalar.activation(hidden[:], proj[:], ACT.Tanh, bias=bias[:, h : h + 1])
-                nc.sync.dma_start(out[units, tokens], hidden[:])
+                nc.sync.dma_start(out[rows, tokens], hidden[:])

@@ -13,9 +13,10 @@ FLOPS = 2 * E * M * N
 
 BF16, F32, U16 = mybir.dt.bfloat16, mybir.dt.float32, mybir.dt.uint16
 ACT = mybir.ActivationFunctionType
-ADD, MULT = mybir.AluOpType.add, mybir.AluOpType.mult
+ADD, MULT, MAX = mybir.AluOpType.add, mybir.AluOpType.mult, mybir.AluOpType.max
 X = mybir.AxisListType.X
-WARM_UP = 3
+FAR_BELOW = 2.0**127
+WARM_UP = 1
 
 
 def tile_deltatemporalmodel_kernel(tc, table, w, b, offs, out):
@@ -48,36 +49,44 @@ def tile_deltatemporalmodel_kernel(tc, table, w, b, offs, out):
 
         identity = held.tile([P, P], F32, name="identity")
         make_identity(nc, identity[:])
-        pairs = held.tile([P, 2 * QUAD], F32, name="pairs")
-        nc.vector.tensor_tensor(
-            pairs[:], identity[:, 0 : 2 * QUAD], identity[:, 2 * QUAD : 4 * QUAD], ADD
-        )
         own = held.tile([P, QUAD], F32, name="own")
-        nc.vector.tensor_tensor(own[:], pairs[:, 0:QUAD], pairs[:, QUAD : 2 * QUAD], ADD)
+        nc.vector.tensor_reduce(own[:], identity[:].rearrange("p (q n) -> p n q", n=QUAD), X, ADD)
+        mask = held.tile([P, WIDEST, QUAD], BF16, name="mask")
+        nc.vector.tensor_scalar(
+            mask[:], own[:].unsqueeze(1).to_broadcast([P, WIDEST, QUAD]), -1.0, FAR_BELOW, ADD, MULT
+        )
+        identity_bf16 = held.tile([P, P], BF16, name="identity_bf16")
+        nc.vector.tensor_copy(identity_bf16[:], identity[:])
+
+        grams = []
+        for unit in units:
+            gram = psum.tile([P, BANK], F32, name="gram", tag="bank")
+            columns = (unit.stop - unit.start) // P * QUAD
+            nc.tensor.matmul(
+                gram[:, 0:columns], identity_bf16[:],
+                mask[:].rearrange("p g n -> p (g n)")[:, 0:columns], start=True, stop=False,
+            )
+            grams.append(gram)
 
         lengths = held.tile([P, S // P], F32, name="lengths")
         inv = held.tile([P, S // P], F32, name="inv")
         scaled = held.tile([P, S], BF16, name="scaled")
 
-        def measure(unit):
+        def measure(unit, gram):
             groups = range(unit.start // P, unit.stop // P)
-            gram = psum.tile([P, BANK // QUAD, QUAD], F32, name="gram", tag="bank")
             for place, g in enumerate(groups):
                 for q in range(P // QUAD):
                     words = raw[:, g * P + q * QUAD : g * P + (q + 1) * QUAD]
                     nc.tensor.matmul(
-                        gram[q * QUAD : (q + 1) * QUAD, place, :], words, words, start=True, stop=True
+                        gram[q * QUAD : (q + 1) * QUAD, place * QUAD : (place + 1) * QUAD],
+                        words, words, start=False, stop=place == len(groups) - 1,
                     )
-            picked = work.tile([P, WIDEST, QUAD], F32, name="picked")
-            diagonal = picked[:, 0 : len(groups), :]
-            nc.vector.tensor_tensor(
-                diagonal,
-                gram[:, 0 : len(groups), :],
-                own[:].unsqueeze(1).to_broadcast([P, len(groups), QUAD]),
-                MULT,
-            )
             columns = slice(groups.start, groups.stop)
-            nc.vector.tensor_reduce(lengths[:, columns], diagonal, X, ADD)
+            nc.vector.tensor_reduce(
+                lengths[:, columns],
+                gram[:, 0 : len(groups) * QUAD].rearrange("p (g n) -> p g n", n=QUAD),
+                X, MAX,
+            )
             nc.scalar.activation(inv[:, columns], lengths[:, columns], ACT.Abs_reciprocal_sqrt)
 
         def scale(unit):
@@ -98,8 +107,8 @@ def tile_deltatemporalmodel_kernel(tc, table, w, b, offs, out):
                 else:
                     nc.vector.tensor_tensor(scaled[:, words], raw[:, words], spread[:], MULT)
 
-        for unit in units:
-            measure(unit)
+        for unit, gram in zip(units, grams):
+            measure(unit, gram)
         for unit in units:
             scale(unit)
 

@@ -7,13 +7,13 @@ BANK = 512
 BANKS = 8
 QUAD = 32
 UNITS = (512, 1024, 1024, 1024, 512)
-WIDEST = max(UNITS) // P
 GPSIMD_BLOCKS = (1, 3)
 FLOPS = 2 * E * M * N
 
 BF16, F32, U16 = mybir.dt.bfloat16, mybir.dt.float32, mybir.dt.uint16
 ACT = mybir.ActivationFunctionType
-ADD, MULT, MAX = mybir.AluOpType.add, mybir.AluOpType.mult, mybir.AluOpType.max
+MULT, MAX = mybir.AluOpType.mult, mybir.AluOpType.max
+NOT_EQUAL = mybir.AluOpType.not_equal
 X = mybir.AxisListType.X
 FAR_BELOW = 2.0**127
 WARM_UP = 1
@@ -47,24 +47,26 @@ def tile_deltatemporalmodel_kernel(tc, table, w, b, offs, out):
         for i in range(WARM_UP):
             nc.tensor.matmul(unread[:, 0:P], ones[:], ones[:], start=True, stop=True)
 
-        identity = held.tile([P, P], F32, name="identity")
-        make_identity(nc, identity[:])
-        own = held.tile([P, QUAD], F32, name="own")
-        nc.vector.tensor_reduce(own[:], identity[:].rearrange("p (q n) -> p n q", n=QUAD), X, ADD)
-        mask = held.tile([P, WIDEST, QUAD], BF16, name="mask")
-        nc.vector.tensor_scalar(
-            mask[:], own[:].unsqueeze(1).to_broadcast([P, WIDEST, QUAD]), -1.0, FAR_BELOW, ADD, MULT
-        )
         identity_bf16 = held.tile([P, P], BF16, name="identity_bf16")
-        nc.vector.tensor_copy(identity_bf16[:], identity[:])
+        make_identity(nc, identity_bf16[:])
+        far_below = held.tile([P, P // QUAD, QUAD], BF16, name="far_below")
+        nc.vector.memset(far_below[:], -FAR_BELOW)
+        nc.gpsimd.affine_select(
+            out=far_below[:], in_=far_below[:], compare_op=NOT_EQUAL, fill=0.0,
+            base=0, pattern=[[0, P // QUAD], [-1, QUAD]], channel_multiplier=1,
+        )
+        identity = held.tile([P, P], F32, name="identity")
+        nc.vector.tensor_copy(identity[:], identity_bf16[:])
 
         grams = []
         for unit in units:
-            gram = psum.tile([P, BANK], F32, name="gram", tag="bank")
-            columns = (unit.stop - unit.start) // P * QUAD
+            groups = (unit.stop - unit.start) // P
+            gram = psum.tile([P, BANK // QUAD, QUAD], F32, name="gram", tag="bank")
             nc.tensor.matmul(
-                gram[:, 0:columns], identity_bf16[:],
-                mask[:].rearrange("p g n -> p (g n)")[:, 0:columns], start=True, stop=False,
+                gram[:, 0:groups, :],
+                far_below[:].rearrange("p q n -> p (q n)"),
+                identity_bf16[:, 0:QUAD].unsqueeze(1).to_broadcast([P, groups, QUAD]),
+                start=True, stop=False,
             )
             grams.append(gram)
 
@@ -78,13 +80,13 @@ def tile_deltatemporalmodel_kernel(tc, table, w, b, offs, out):
                 for q in range(P // QUAD):
                     words = raw[:, g * P + q * QUAD : g * P + (q + 1) * QUAD]
                     nc.tensor.matmul(
-                        gram[q * QUAD : (q + 1) * QUAD, place * QUAD : (place + 1) * QUAD],
+                        gram[q * QUAD : (q + 1) * QUAD, place, :],
                         words, words, start=False, stop=place == len(groups) - 1,
                     )
             columns = slice(groups.start, groups.stop)
             nc.vector.tensor_reduce(
                 lengths[:, columns],
-                gram[:, 0 : len(groups) * QUAD].rearrange("p (g n) -> p g n", n=QUAD),
+                gram[:, 0 : len(groups), :],
                 X, MAX,
             )
             nc.scalar.activation(inv[:, columns], lengths[:, columns], ACT.Abs_reciprocal_sqrt)

@@ -25,7 +25,7 @@ def tile_deltatemporalmodel_kernel(tc, table, w, b, offs, out):
     with (
         tc.tile_pool(name="held", bufs=1) as held,
         tc.tile_pool(name="work", bufs=2) as work,
-        tc.tile_pool(name="results", bufs=4) as results,
+        tc.tile_pool(name="results", bufs=8) as results,
         tc.psum_pool(name="psum", bufs=BANKS) as psum,
     ):
         raw = held.tile([P, S], BF16, name="raw")
@@ -115,7 +115,6 @@ def tile_deltatemporalmodel_kernel(tc, table, w, b, offs, out):
             scale(unit)
 
         for t in range(N // BANK):
-            tokens = slice(t * BANK, (t + 1) * BANK)
             piece = offsets[:, t * (BANK // 16) : (t + 1) * (BANK // 16)]
             for h in range(M // P):
                 rows = slice(h * P, (h + 1) * P)
@@ -123,6 +122,9 @@ def tile_deltatemporalmodel_kernel(tc, table, w, b, offs, out):
                 nc.tensor.matmul(
                     proj[:], weights[:, rows], scaled[:].indirect(piece), start=True, stop=True
                 )
-                hidden = results.tile([P, BANK], F32, name="hidden")
-                nc.scalar.activation(hidden[:], proj[:], ACT.Tanh, bias=bias[:, h : h + 1])
-                nc.sync.dma_start(out[rows, tokens], hidden[:])
+                for first in range(0, BANK, BANK // 2):
+                    part = slice(first, first + BANK // 2)
+                    tokens = slice(t * BANK + part.start, t * BANK + part.stop)
+                    hidden = results.tile([P, BANK // 2], F32, name="hidden")
+                    nc.scalar.activation(hidden[:], proj[:, part], ACT.Tanh, bias=bias[:, h : h + 1])
+                    nc.sync.dma_start(out[rows, tokens], hidden[:])

@@ -16,7 +16,7 @@ MULT, MAX = mybir.AluOpType.mult, mybir.AluOpType.max
 NOT_EQUAL = mybir.AluOpType.not_equal
 X = mybir.AxisListType.X
 FAR_BELOW = 2.0**127
-WARM_UP = 1
+WARM_UP = 2
 
 
 def tile_deltatemporalmodel_kernel(tc, table, w, b, offs, out):
@@ -38,14 +38,17 @@ def tile_deltatemporalmodel_kernel(tc, table, w, b, offs, out):
         bias = held.tile([P, M // P], F32, name="bias")
         nc.sync.dma_start(bias[:], b.rearrange("(h p) one -> p (h one)", p=P))
 
-        ones = held.tile([P, P], F32, name="ones")
+        ones = held.tile([P, 1], BF16, name="ones")
         nc.vector.memset(ones[:], 1.0)
         early = held.tile([P, 1], F32, name="early")
-        nc.scalar.activation(early[:], ones[:, 0:1], ACT.Abs_reciprocal_sqrt)
+        nc.scalar.activation(early[:], ones[:], ACT.Abs_reciprocal_sqrt)
 
         unread = psum.tile([P, BANK], F32, name="unread", tag="bank")
         for i in range(WARM_UP):
-            nc.tensor.matmul(unread[:, 0:P], ones[:], ones[:], start=True, stop=True)
+            nc.tensor.matmul(
+                unread[:], ones[:].to_broadcast([P, P]), ones[:].to_broadcast([P, BANK]),
+                start=True, stop=True,
+            )
 
         identity_bf16 = held.tile([P, P], BF16, name="identity_bf16")
         make_identity(nc, identity_bf16[:])

@@ -7,7 +7,8 @@ BANK = 512
 BANKS = 8
 QUAD = 32
 UNITS = (512, 1024, 1024, 1024, 512)
-GPSIMD_BLOCKS = (1, 3)
+GPSIMD_BLOCKS = (0, 2)
+SCALAR_BLOCK = 4
 FLOPS = 2 * E * M * N
 
 BF16, F32, U16 = mybir.dt.bfloat16, mybir.dt.float32, mybir.dt.uint16
@@ -94,8 +95,33 @@ def tile_deltatemporalmodel_kernel(tc, table, w, b, offs, out):
             )
             nc.scalar.activation(inv[:, columns], lengths[:, columns], ACT.Abs_reciprocal_sqrt)
 
+        turned = held.tile([P, BANK // P, P], BF16, name="turned")
+
+        def turn_and_scale(first):
+            upright = psum.tile([P, BANK // P, P], BF16, name="upright", tag="bank")
+            for place in range(BANK // P):
+                words = raw[:, first + place * P : first + (place + 1) * P]
+                nc.tensor.transpose(upright[:, place, :], words, identity_bf16[:])
+            for place in range(BANK // P):
+                g = first // P + place
+                nc.scalar.activation(
+                    turned[:, place, :], upright[:, place, :], ACT.Copy, scale=inv[:, g : g + 1]
+                )
+
+        def turn_back():
+            flat = psum.tile([P, BANK // P, P], BF16, name="flat", tag="bank")
+            for place in range(BANK // P):
+                nc.tensor.transpose(flat[:, place, :], turned[:, place, :], identity_bf16[:])
+            first = SCALAR_BLOCK * BANK
+            nc.scalar.copy(
+                scaled[:, first : first + BANK], flat[:].rearrange("p g n -> p (g n)")
+            )
+
         def scale(unit):
             for first in range(unit.start, unit.stop, BANK):
+                if first // BANK == SCALAR_BLOCK:
+                    turn_and_scale(first)
+                    continue
                 spread = psum.tile([P, BANK], F32, name="spread", tag="bank")
                 for place in range(BANK // P):
                     g = first // P + place
@@ -116,6 +142,7 @@ def tile_deltatemporalmodel_kernel(tc, table, w, b, offs, out):
             measure(unit, gram)
         for unit in units:
             scale(unit)
+        turn_back()
 
         for t in range(N // BANK):
             piece = offsets[:, t * (BANK // 16) : (t + 1) * (BANK // 16)]

@@ -17,7 +17,6 @@ MULT, MAX = mybir.AluOpType.mult, mybir.AluOpType.max
 NOT_EQUAL = mybir.AluOpType.not_equal
 X = mybir.AxisListType.X
 FAR_BELOW = 2.0**127
-WARM_UP = 2
 
 
 def tile_deltatemporalmodel_kernel(tc, table, w, b, offs, out):
@@ -43,13 +42,6 @@ def tile_deltatemporalmodel_kernel(tc, table, w, b, offs, out):
         nc.vector.memset(ones[:], 1.0)
         early = held.tile([P, 1], F32, name="early")
         nc.scalar.activation(early[:], ones[:], ACT.Abs_reciprocal_sqrt)
-
-        unread = psum.tile([P, BANK], F32, name="unread", tag="bank")
-        for i in range(WARM_UP):
-            nc.tensor.matmul(
-                unread[:], ones[:].to_broadcast([P, P]), ones[:].to_broadcast([P, BANK]),
-                start=True, stop=True,
-            )
 
         identity_bf16 = held.tile([P, P], BF16, name="identity_bf16")
         make_identity(nc, identity_bf16[:])

@@ -13,8 +13,7 @@ FLOPS = 2 * E * M * N
 
 BF16, F32, U16 = mybir.dt.bfloat16, mybir.dt.float32, mybir.dt.uint16
 ACT = mybir.ActivationFunctionType
-MULT, MAX = mybir.AluOpType.mult, mybir.AluOpType.max
-NOT_EQUAL = mybir.AluOpType.not_equal
+ADD, MULT, MAX = mybir.AluOpType.add, mybir.AluOpType.mult, mybir.AluOpType.max
 X = mybir.AxisListType.X
 FAR_BELOW = 2.0**127
 
@@ -46,10 +45,10 @@ def tile_deltatemporalmodel_kernel(tc, table, w, b, offs, out):
         identity_bf16 = held.tile([P, P], BF16, name="identity_bf16")
         make_identity(nc, identity_bf16[:])
         far_below = held.tile([P, P // QUAD, QUAD], BF16, name="far_below")
-        nc.vector.memset(far_below[:], -FAR_BELOW)
-        nc.gpsimd.affine_select(
-            out=far_below[:], in_=far_below[:], compare_op=NOT_EQUAL, fill=0.0,
-            base=0, pattern=[[0, P // QUAD], [-1, QUAD]], channel_multiplier=1,
+        nc.vector.tensor_scalar(
+            far_below[:],
+            identity_bf16[:, 0:QUAD].unsqueeze(1).to_broadcast([P, P // QUAD, QUAD]),
+            -1.0, FAR_BELOW, ADD, MULT,
         )
         identity = held.tile([P, P], F32, name="identity")
         nc.vector.tensor_copy(identity[:], identity_bf16[:])

import concourse.mybir as mybir
from concourse.masks import make_identity

E, S, M, N = 128, 4096, 256, 1024
P = 128
BANK = 512
BANKS = 8
QUAD = 32
UNITS = (512, 1024, 1024, 1024, 512)
GPSIMD_BLOCKS = (0, 2)
SCALAR_BLOCK = 4
FLOPS = 2 * E * M * N

BF16, F32, U16 = mybir.dt.bfloat16, mybir.dt.float32, mybir.dt.uint16
ACT = mybir.ActivationFunctionType
ADD, MULT, MAX = mybir.AluOpType.add, mybir.AluOpType.mult, mybir.AluOpType.max
X = mybir.AxisListType.X
FAR_BELOW = 2.0**127


def tile_deltatemporalmodel_kernel(tc, table, w, b, offs, out):
    nc = tc.nc
    units = [slice(sum(UNITS[:u]), sum(UNITS[: u + 1])) for u in range(len(UNITS))]
    with (
        tc.tile_pool(name="held", bufs=1) as held,
        tc.tile_pool(name="work", bufs=2) as work,
        tc.tile_pool(name="results", bufs=8) as results,
        tc.psum_pool(name="psum", bufs=BANKS) as psum,
    ):
        raw = held.tile([P, S], BF16, name="raw")
        for words in units:
            nc.sync.dma_start(raw[:, words], table[:, words])
        offsets = held.tile([P, N // 16], U16, name="offsets")
        nc.sync.dma_start(offsets[:], offs)
        weights = held.tile([P, M], BF16, name="weights")
        nc.sync.dma_start(weights[:], w)
        bias = held.tile([P, M // P], F32, name="bias")
        nc.sync.dma_start(bias[:], b.rearrange("(h p) one -> p (h one)", p=P))

        ones = held.tile([P, 1], BF16, name="ones")
        nc.vector.memset(ones[:], 1.0)
        early = held.tile([P, 1], F32, name="early")
        nc.scalar.activation(early[:], ones[:], ACT.Abs_reciprocal_sqrt)

        identity_bf16 = held.tile([P, P], BF16, name="identity_bf16")
        make_identity(nc, identity_bf16[:])
        far_below = held.tile([P, P // QUAD, QUAD], BF16, name="far_below")
        nc.vector.tensor_scalar(
            far_below[:],
            identity_bf16[:, 0:QUAD].unsqueeze(1).to_broadcast([P, P // QUAD, QUAD]),
            -1.0, FAR_BELOW, ADD, MULT,
        )
        identity = held.tile([P, P], F32, name="identity")
        nc.vector.tensor_copy(identity[:], identity_bf16[:])

        grams = []
        for unit in units:
            groups = (unit.stop - unit.start) // P
            gram = psum.tile([P, BANK // QUAD, QUAD], F32, name="gram", tag="bank")
            nc.tensor.matmul(
                gram[:, 0:groups, :],
                far_below[:].rearrange("p q n -> p (q n)"),
                identity_bf16[:, 0:QUAD].unsqueeze(1).to_broadcast([P, groups, QUAD]),
                start=True, stop=False,
            )
            grams.append(gram)

        lengths = held.tile([P, S // P], F32, name="lengths")
        inv = held.tile([P, S // P], F32, name="inv")
        scaled = held.tile([P, S], BF16, name="scaled")

        def measure(unit, gram):
            groups = range(unit.start // P, unit.stop // P)
            for place, g in enumerate(groups):
                for q in range(P // QUAD):
                    words = raw[:, g * P + q * QUAD : g * P + (q + 1) * QUAD]
                    nc.tensor.matmul(
                        gram[q * QUAD : (q + 1) * QUAD, place, :],
                        words, words, start=False, stop=place == len(groups) - 1,
                    )
            columns = slice(groups.start, groups.stop)
            nc.vector.tensor_reduce(
                lengths[:, columns],
                gram[:, 0 : len(groups), :],
                X, MAX,
            )
            nc.scalar.activation(inv[:, columns], lengths[:, columns], ACT.Abs_reciprocal_sqrt)

        turned = held.tile([P, BANK // P, P], BF16, name="turned")

        def turn_and_scale(first):
            upright = psum.tile([P, BANK // P, P], BF16, name="upright", tag="bank")
            for place in range(BANK // P):
                words = raw[:, first + place * P : first + (place + 1) * P]
                nc.tensor.transpose(upright[:, place, :], words, identity_bf16[:])
            for place in range(BANK // P):
                g = first // P + place
                nc.scalar.activation(
                    turned[:, place, :], upright[:, place, :], ACT.Copy, scale=inv[:, g : g + 1]
                )

        def turn_back():
            flat = psum.tile([P, BANK // P, P], BF16, name="flat", tag="bank")
            for place in range(BANK // P):
                nc.tensor.transpose(flat[:, place, :], turned[:, place, :], identity_bf16[:])
            first = SCALAR_BLOCK * BANK
            nc.scalar.copy(
                scaled[:, first : first + BANK], flat[:].rearrange("p g n -> p (g n)")
            )

        def scale(unit):
            for first in range(unit.start, unit.stop, BANK):
                if first // BANK == SCALAR_BLOCK:
                    turn_and_scale(first)
                    continue
                spread = psum.tile([P, BANK], F32, name="spread", tag="bank")
                for place in range(BANK // P):
                    g = first // P + place
                    nc.tensor.transpose(
                        spread[:, place * P : (place + 1) * P],
                        inv[:, g : g + 1].to_broadcast([P, P]),
                        identity[:],
                    )
                words = slice(first, first + BANK)
                if first // BANK in GPSIMD_BLOCKS:
                    copied = work.tile([P, BANK], F32, name="copied")
                    nc.scalar.copy(copied[:], spread[:])
                    nc.gpsimd.tensor_tensor(scaled[:, words], raw[:, words], copied[:], MULT)
                else:
                    nc.vector.tensor_tensor(scaled[:, words], raw[:, words], spread[:], MULT)

        for unit, gram in zip(units, grams):
            measure(unit, gram)
        for unit in units:
            scale(unit)
        turn_back()

        for t in range(N // BANK):
            piece = offsets[:, t * (BANK // 16) : (t + 1) * (BANK // 16)]
            for h in range(M // P):
                rows = slice(h * P, (h + 1) * P)
                proj = psum.tile([P, BANK], F32, name="proj", tag="bank")
                nc.tensor.matmul(
                    proj[:], weights[:, rows], scaled[:].indirect(piece), start=True, stop=True
                )
                for first in range(0, BANK, BANK // 2):
                    part = slice(first, first + BANK // 2)
                    tokens = slice(t * BANK + part.start, t * BANK + part.stop)
                    hidden = results.tile([P, BANK // 2], F32, name="hidden")
                    nc.scalar.activation(hidden[:], proj[:, part], ACT.Tanh, bias=bias[:, h : h + 1])
                    nc.sync.dma_start(out[rows, tokens], hidden[:])
